import numpy as np
import ml_dtypes


def mxq(x, axis, fmt="e4m3"):
    dtype, down = {"e4m3": (ml_dtypes.float8_e4m3fn, 7), "e5m2": (ml_dtypes.float8_e5m2, 14)}[fmt]
    v = np.moveaxis(np.asarray(x, np.float32).astype(ml_dtypes.bfloat16).astype(np.float64), axis, -1)
    blocks = v.reshape(v.shape[:-1] + (-1, 32))
    amax = np.abs(blocks).max(-1, keepdims=True)
    byte = np.maximum(np.where(amax > 0, np.frexp(amax)[1] - 1 + 127, 0) - down, 1)
    scale = np.exp2(byte - 127.0)
    codes = (blocks / scale).astype(np.float32).astype(dtype).astype(np.float64)
    return np.moveaxis((codes * scale).reshape(v.shape), -1, axis)


WIDE = False


def mx_kscale(k):
    if not WIDE:
        return np.ones(k)
    levels = np.array([10, -10, 5, -5, 0])
    a = np.random.permutation(np.resize(levels, k // 512 * 4)).reshape(k // 512, 4)
    idx = np.arange(k)
    return np.exp2(a[idx // 512, idx % 128 // 32])


BF16 = ml_dtypes.bfloat16


def bf(x):
    return np.asarray(x, np.float32).astype(BF16)


def f64(x):
    return np.asarray(x).astype(np.float64)


T, B, I, H = 64, 128, 512, 128


def sigmoid(v):
    return 1.0 / (1.0 + np.exp(-v))


def setup_inputs():
    s = mx_kscale(I)
    return {"input_seq": bf(np.random.standard_normal((T, B, I)) * s),
            "W_ih": bf(np.random.standard_normal((3 * H, I)) / np.sqrt(I) / s[None, :]),
            "b_ih": bf(np.random.standard_normal(3 * H) * 0.3),
            "gh": bf(np.random.standard_normal((B, 3 * H)) * 0.5)}


def reference(input_seq, W_ih, b_ih, gh):
    gi = (mxq(f64(input_seq), 2, "e4m3") @ mxq(f64(W_ih), 1, "e4m3").T) + f64(b_ih)
    g = f64(gh)
    i_r, i_z, i_n = gi[..., :H], gi[..., H:2 * H], gi[..., 2 * H:]
    h_r, h_z, h_n = g[..., :H], g[..., H:2 * H], g[..., 2 * H:]
    r = sigmoid(i_r + h_r)
    z = sigmoid(i_z + h_z)
    n = np.tanh(i_n + r * h_n)
    h = (1.0 - z) * n
    return np.transpose(h, (1, 0, 2))

@@ -1,0 +1,254 @@
+from contextlib import ExitStack
+
+import concourse.mybir as mybir
+from concourse.masks import make_identity
+
+F32 = mybir.dt.float32
+BF16 = mybir.dt.bfloat16
+U32 = mybir.dt.uint32
+U8 = mybir.dt.uint8
+FP8X4 = mybir.dt.float8_e4m3fn_x4
+ACT = mybir.ActivationFunctionType
+ALU = mybir.AluOpType
+
+T, B, I, H = 64, 128, 512, 128
+P = 128
+FLOPS = 2 * T * B * I * 3 * H
+
+NU = 16
+CHUNKS = [4, 4, 8, 8, 8, 8, 8, 8, 8]
+MANUAL = True
+MULT_ON_GPSIMD = True
+
+
+def tile_grucellmodel_pa_t_kernel(tc, input_seq, W_ih, b_ih, gh, out):
+    nc = tc.nc
+    with ExitStack() as ctx:
+        const = ctx.enter_context(tc.tile_pool(name="const", bufs=1))
+        xpool = ctx.enter_context(tc.tile_pool(name="xpool", bufs=1))
+        gpool = ctx.enter_context(tc.tile_pool(name="gpool", bufs=3))
+        work = ctx.enter_context(tc.tile_pool(name="work", bufs=3))
+        psx = ctx.enter_context(tc.psum_pool(name="psx", bufs=2))
+        psg = ctx.enter_context(tc.psum_pool(name="psg", bufs=5))
+        pso = ctx.enter_context(tc.psum_pool(name="pso", bufs=1))
+        if MANUAL:
+            ctx.enter_context(tc.manual_schedule())
+
+        ghb = const.tile([P, 512], BF16)
+        nc.vector.memset(ghb[:, 384:512], 0.0)
+        nc.scalar.dma_start(out=ghb[:, 0:384], in_=gh)
+        nc.scalar.dma_start(out=ghb[0:3, 384:512], in_=b_ih.rearrange("(g h) -> g h", g=3))
+        w_sb = const.tile([P, 3 * I], BF16)
+        nc.scalar.dma_start(
+            out=w_sb[:].rearrange("p (g k) -> p g k", g=3),
+            in_=W_ih.rearrange("(g p) k -> p g k", g=3),
+        )
+        xflat = input_seq.rearrange("t b k -> (t b k)").rearrange("(p f) -> p f", p=P)
+        unit_src = []
+        bb0 = 0
+        for c, nbb in enumerate(CHUNKS):
+            xc = xpool.tile([P, nbb * I], BF16, name="x%d" % c)
+            nc.sync.dma_start(out=xc[:], in_=xflat[:, bb0 * I : (bb0 + nbb) * I])
+            for s in range(nbb // 4):
+                unit_src.append((xc[:].bitcast(F32), s * 4 * 256))
+            bb0 += nbb
+        out_view = out.rearrange("b t h -> (b t h)").rearrange(
+            "(q j i f) -> j i q f", q=2, j=NU, i=P
+        )
+
+        ident = const.tile([P, P], F32)
+        make_identity(nc, ident[:])
+        perm = const.tile([P, P], F32)
+        nc.vector.tensor_copy(
+            out=perm[:].rearrange("p (q l h) -> p q l h", q=2, l=2),
+            in_=ident[:].rearrange("p (h l q) -> p q l h", q=2, l=2),
+        )
+
+        ghf = const.tile([P, 512], F32)
+        nc.vector.tensor_copy(out=ghf[:], in_=ghb[:])
+        pgh = psg.tile([P, 512], F32, tag="gate")
+        for g in range(4):
+            nc.tensor.transpose(pgh[:, g * P : (g + 1) * P], ghf[:, g * P : (g + 1) * P], ident[:])
+
+        ww = w_sb[:].bitcast(F32)
+        pwa = psg.tile([P, 512], F32, tag="gate")
+        pwb = psg.tile([P, 512], F32, tag="gate")
+        for g in range(3):
+            for u in range(2):
+                dst = pwa[:, (2 * g + u) * P : (2 * g + u + 1) * P] if g < 2 else pwb[:, u * P : (u + 1) * P]
+                nc.tensor.transpose(dst, ww[:, g * 256 + u * P : g * 256 + (u + 1) * P], ident[:])
+        wgrouped = const.tile([P, 3 * I], BF16, align_bytes=64)
+        wgw = wgrouped[:].bitcast(F32)
+        nc.vector.tensor_copy(
+            out=wgw[:, 0:512].rearrange("p (c n u) -> p c n u", c=2, u=2),
+            in_=pwa[:].rearrange("p (c u n) -> p c n u", c=2, u=2),
+        )
+        nc.scalar.copy(
+            out=wgw[:, 512:768].rearrange("p (n u) -> p n u", u=2),
+            in_=pwb[:, 0:256].rearrange("p (u n) -> p n u", u=2),
+        )
+        wcodes = const.tile([P, 3 * P], U32, align_bytes=64)
+        wscales = const.tile([P, 3 * P], U8, align_bytes=64)
+
+        banks = {}
+        grouped = {}
+        codes = {}
+        gates = {}
+        acts = {}
+        res = {}
+        pout = {}
+
+        def transposes(j):
+            xw, off = unit_src[j]
+            pair = []
+            for half in range(2):
+                xt = psx.tile([P, 512], F32, tag="xt")
+                for c in range(2):
+                    for u in range(2):
+                        w0 = off + (2 * half + c) * 256 + u * P
+                        nc.tensor.transpose(
+                            xt[:, (2 * c + u) * P : (2 * c + u + 1) * P], xw[:, w0 : w0 + P], perm[:]
+                        )
+                pair.append(xt)
+            banks[j] = pair
+
+        def copies(j, engines):
+            gr = gpool.tile([P, 2048], BF16, tag="grouped", align_bytes=64)
+            gw = gr[:].bitcast(F32)
+            for half in range(2):
+                dst = gw[:, half * 512 : (half + 1) * 512].rearrange("p (c n u) -> p c n u", c=2, u=2)
+                src = banks[j][half][:].rearrange("p (c u n) -> p c n u", c=2, u=2)
+                if engines[half] == "v":
+                    nc.vector.tensor_copy(out=dst, in_=src)
+                else:
+                    nc.scalar.copy(out=dst, in_=src)
+            grouped[j] = gr
+
+        def quantise(j):
+            cd = gpool.tile([P, 512], U32, tag="codes", align_bytes=64)
+            sc = gpool.tile([P, 512], U8, tag="scales", align_bytes=64)
+            nc.vector.quantize_mx(out=cd[:].bitcast(FP8X4), scales=sc[:], in_=grouped[j][:])
+            codes[j] = (cd, sc)
+
+        def passes(j):
+            cd, sc = codes[j]
+            trio = []
+            for g in range(3):
+                pg = psg.tile([P, 512], F32, tag="gate")
+                nc.tensor.matmul_mx(
+                    out=pg[:],
+                    lhsT=wcodes[:, g * P : (g + 1) * P].bitcast(FP8X4),
+                    lhsT_scale=wscales[:, g * P : (g + 1) * P],
+                    rhs=cd[:].bitcast(FP8X4),
+                    rhs_scale=sc[:],
+                    start=True,
+                    stop=True,
+                )
+                trio.append(pg)
+            gates[j] = trio
+
+        def split(ap):
+            return ap.rearrange("p (l h) -> p l h", l=2)
+
+        def placed(tile_ap):
+            return tile_ap.rearrange("p (q l c h) -> p q l c h", q=2, l=2, c=4)
+
+        def reset_and_candidate(j):
+            pr, pz, pn = gates[j]
+            r = work.tile([P, 512], F32, tag="r")
+            v = work.tile([P, 512], F32, tag="v")
+            v5 = placed(v[:])
+            for c in range(4):
+                for q in range(2):
+                    b = q * 64 + 4 * j + c
+                    c0 = c * P + q * 64
+                    nc.scalar.activation(
+                        out=r[:, c0 : c0 + 64], in_=pr[:, c0 : c0 + 64], func=ACT.Sigmoid,
+                        bias=g_r[:, b : b + 1], scale=1.0,
+                    )
+                    nc.vector.scalar_tensor_tensor(
+                        out=v5[:, q, :, c, :], in0=split(r[:, c0 : c0 + 64]), scalar=h_n[:, b : b + 1],
+                        in1=split(pn[:, c0 : c0 + 64]), op0=ALU.mult, op1=ALU.add,
+                    )
+            acts[j] = [v]
+
+        def update(j):
+            pz = gates[j][1]
+            zc = work.tile([P, 512], F32, tag="zc")
+            z5 = placed(zc[:])
+            for c in range(4):
+                for q in range(2):
+                    b = q * 64 + 4 * j + c
+                    c0 = c * P + q * 64
+                    nc.scalar.activation(
+                        out=z5[:, q, :, c, :], in_=split(pz[:, c0 : c0 + 64]), func=ACT.Sigmoid,
+                        bias=g_zn[:, b : b + 1], scale=-1.0,
+                    )
+            acts[j].append(zc)
+
+        def candidate_and_product(j):
+            v, zc = acts[j]
+            n = work.tile([P, 512], F32, tag="n")
+            nc.scalar.activation(out=n[:], in_=v[:], func=ACT.Tanh, bias=bcol[:, 2:3], scale=1.0)
+            rs = work.tile([P, 512], F32, tag="rs")
+            if MULT_ON_GPSIMD:
+                nc.gpsimd.tensor_tensor(out=rs[:], in0=zc[:], in1=n[:], op=ALU.mult)
+            else:
+                nc.vector.tensor_tensor(out=rs[:], in0=zc[:], in1=n[:], op=ALU.mult)
+            res[j] = rs
+
+        def back_transposes(j):
+            po = pso.tile([P, 512], F32, tag="po")
+            for q in range(4):
+                nc.tensor.transpose(po[:, q * P : (q + 1) * P], res[j][:, q * P : (q + 1) * P], ident[:])
+            pout[j] = po
+
+        def store(j):
+            osb = work.tile([P, 512], F32, tag="osb")
+            nc.scalar.copy(out=osb[:], in_=pout[j][:])
+            nc.sync.dma_start(out=out_view[j], in_=osb[:].rearrange("p (q f) -> p q f", q=2))
+
+        transposes(0)
+        copies(0, "vs")
+        for g in range(3):
+            nc.vector.quantize_mx(
+                out=wcodes[:, g * P : (g + 1) * P].bitcast(FP8X4),
+                scales=wscales[:, g * P : (g + 1) * P],
+                in_=wgrouped[:, g * I : (g + 1) * I],
+            )
+        quantise(0)
+        transposes(1)
+        passes(0)
+        bcol = const.tile([P, 4], F32)
+        nc.vector.tensor_copy(out=bcol[:], in_=pgh[:, 384:388])
+        g_r = const.tile([P, P], F32)
+        nc.vector.tensor_scalar(out=g_r[:], in0=pgh[:, 0:128], scalar1=bcol[:, 0:1], scalar2=None, op0=ALU.add)
+        g_zn = const.tile([P, P], F32)
+        nc.vector.tensor_scalar(
+            out=g_zn[:], in0=pgh[:, 128:256], scalar1=bcol[:, 1:2], scalar2=-1.0, op0=ALU.add, op1=ALU.mult
+        )
+        h_n = const.tile([P, P], F32)
+        nc.vector.tensor_copy(out=h_n[:], in_=pgh[:, 256:384])
+        copies(1, "vs")
+        transposes(2)
+        quantise(1)
+        copies(2, "vs")
+
+        for i in range(NU + 1):
+            if i + 3 < NU:
+                transposes(i + 3)
+            if i >= 1:
+                back_transposes(i - 1)
+            if i + 1 < NU:
+                passes(i + 1)
+            if i < NU:
+                reset_and_candidate(i)
+                update(i)
+            if i + 2 < NU:
+                quantise(i + 2)
+            if i + 3 < NU:
+                copies(i + 3, "vv")
+            if i < NU:
+                candidate_and_product(i)
+            if i >= 1:
+                store(i - 1)

@@ -16,9 +16,8 @@ P = 128
 FLOPS = 2 * T * B * I * 3 * H
 
 NU = 16
-CHUNKS = [4, 4, 8, 8, 8, 8, 8, 8, 8]
-MANUAL = True
-MULT_ON_GPSIMD = True
+CHUNKS = [2, 2, 4, 8, 8, 8, 8, 8, 8, 8]
+AHEAD = 3
 
 
 def tile_grucellmodel_pa_t_kernel(tc, input_seq, W_ih, b_ih, gh, out):
@@ -26,31 +25,34 @@ def tile_grucellmodel_pa_t_kernel(tc, input_seq, W_ih, b_ih, gh, out):
     with ExitStack() as ctx:
         const = ctx.enter_context(tc.tile_pool(name="const", bufs=1))
         xpool = ctx.enter_context(tc.tile_pool(name="xpool", bufs=1))
-        gpool = ctx.enter_context(tc.tile_pool(name="gpool", bufs=3))
+        gpool = ctx.enter_context(tc.tile_pool(name="gpool", bufs=4))
         work = ctx.enter_context(tc.tile_pool(name="work", bufs=3))
         psx = ctx.enter_context(tc.psum_pool(name="psx", bufs=2))
         psg = ctx.enter_context(tc.psum_pool(name="psg", bufs=5))
         pso = ctx.enter_context(tc.psum_pool(name="pso", bufs=1))
-        if MANUAL:
-            ctx.enter_context(tc.manual_schedule())
+        ctx.enter_context(tc.manual_schedule())
 
         ghb = const.tile([P, 512], BF16)
         nc.vector.memset(ghb[:, 384:512], 0.0)
         nc.scalar.dma_start(out=ghb[:, 0:384], in_=gh)
         nc.scalar.dma_start(out=ghb[0:3, 384:512], in_=b_ih.rearrange("(g h) -> g h", g=3))
+        warm = const.tile([P, 1], F32)
+        nc.vector.memset(warm[:], 0.0)
+        warm2 = const.tile([P, 1], F32)
+        nc.scalar.activation(out=warm2[:], in_=warm[:], func=ACT.Sigmoid)
         w_sb = const.tile([P, 3 * I], BF16)
-        nc.scalar.dma_start(
+        nc.sync.dma_start(
             out=w_sb[:].rearrange("p (g k) -> p g k", g=3),
             in_=W_ih.rearrange("(g p) k -> p g k", g=3),
         )
         xflat = input_seq.rearrange("t b k -> (t b k)").rearrange("(p f) -> p f", p=P)
-        unit_src = []
+        half_src = []
         bb0 = 0
         for c, nbb in enumerate(CHUNKS):
             xc = xpool.tile([P, nbb * I], BF16, name="x%d" % c)
             nc.sync.dma_start(out=xc[:], in_=xflat[:, bb0 * I : (bb0 + nbb) * I])
-            for s in range(nbb // 4):
-                unit_src.append((xc[:].bitcast(F32), s * 4 * 256))
+            for s in range(nbb // 2):
+                half_src.append((xc[:].bitcast(F32), s * 2 * 256))
             bb0 += nbb
         out_view = out.rearrange("b t h -> (b t h)").rearrange(
             "(q j i f) -> j i q f", q=2, j=NU, i=P
@@ -65,7 +67,7 @@ def tile_grucellmodel_pa_t_kernel(tc, input_seq, W_ih, b_ih, gh, out):
         )
 
         ghf = const.tile([P, 512], F32)
-        nc.vector.tensor_copy(out=ghf[:], in_=ghb[:])
+        nc.scalar.copy(out=ghf[:], in_=ghb[:])
         pgh = psg.tile([P, 512], F32, tag="gate")
         for g in range(4):
             nc.tensor.transpose(pgh[:, g * P : (g + 1) * P], ghf[:, g * P : (g + 1) * P], ident[:])
@@ -98,31 +100,31 @@ def tile_grucellmodel_pa_t_kernel(tc, input_seq, W_ih, b_ih, gh, out):
         res = {}
         pout = {}
 
-        def transposes(j):
-            xw, off = unit_src[j]
+        def transposes(j, pool, tag):
             pair = []
             for half in range(2):
-                xt = psx.tile([P, 512], F32, tag="xt")
+                xw, off = half_src[2 * j + half]
+                xt = pool.tile([P, 512], F32, tag=tag)
                 for c in range(2):
                     for u in range(2):
-                        w0 = off + (2 * half + c) * 256 + u * P
+                        w0 = off + c * 256 + u * P
                         nc.tensor.transpose(
                             xt[:, (2 * c + u) * P : (2 * c + u + 1) * P], xw[:, w0 : w0 + P], perm[:]
                         )
                 pair.append(xt)
             banks[j] = pair
 
-        def copies(j, engines):
-            gr = gpool.tile([P, 2048], BF16, tag="grouped", align_bytes=64)
-            gw = gr[:].bitcast(F32)
-            for half in range(2):
-                dst = gw[:, half * 512 : (half + 1) * 512].rearrange("p (c n u) -> p c n u", c=2, u=2)
-                src = banks[j][half][:].rearrange("p (c u n) -> p c n u", c=2, u=2)
-                if engines[half] == "v":
-                    nc.vector.tensor_copy(out=dst, in_=src)
-                else:
-                    nc.scalar.copy(out=dst, in_=src)
-            grouped[j] = gr
+        def copy_half(j, half):
+            if half == 0:
+                gr = gpool.tile([P, 2048], BF16, tag="grouped", align_bytes=64, bufs=3)
+                grouped[j] = gr
+            gw = grouped[j][:].bitcast(F32)
+            dst = gw[:, half * 512 : (half + 1) * 512].rearrange("p (c n u) -> p c n u", c=2, u=2)
+            src = banks[j][half][:].rearrange("p (c u n) -> p c n u", c=2, u=2)
+            if half == 0 and (j == 0 or j % 2 == 1):
+                nc.scalar.copy(out=dst, in_=src)
+            else:
+                nc.vector.tensor_copy(out=dst, in_=src)
 
         def quantise(j):
             cd = gpool.tile([P, 512], U32, tag="codes", align_bytes=64)
@@ -132,8 +134,8 @@ def tile_grucellmodel_pa_t_kernel(tc, input_seq, W_ih, b_ih, gh, out):
 
         def passes(j):
             cd, sc = codes[j]
-            trio = []
-            for g in range(3):
+            trio = {}
+            for g in (0, 2, 1):
                 pg = psg.tile([P, 512], F32, tag="gate")
                 nc.tensor.matmul_mx(
                     out=pg[:],
@@ -144,7 +146,7 @@ def tile_grucellmodel_pa_t_kernel(tc, input_seq, W_ih, b_ih, gh, out):
                     start=True,
                     stop=True,
                 )
-                trio.append(pg)
+                trio[g] = pg
             gates[j] = trio
 
         def split(ap):
@@ -154,8 +156,9 @@ def tile_grucellmodel_pa_t_kernel(tc, input_seq, W_ih, b_ih, gh, out):
             return tile_ap.rearrange("p (q l c h) -> p q l c h", q=2, l=2, c=4)
 
         def reset_and_candidate(j):
-            pr, pz, pn = gates[j]
-            r = work.tile([P, 512], F32, tag="r")
+            pr = gates[j][0]
+            pn = gates[j][2]
+            r = work.tile([P, 512], F32, tag="r", bufs=2)
             v = work.tile([P, 512], F32, tag="v")
             v5 = placed(v[:])
             for c in range(4):
@@ -188,10 +191,10 @@ def tile_grucellmodel_pa_t_kernel(tc, input_seq, W_ih, b_ih, gh, out):
 
         def candidate_and_product(j):
             v, zc = acts[j]
-            n = work.tile([P, 512], F32, tag="n")
+            n = work.tile([P, 512], F32, tag="n", bufs=2)
             nc.scalar.activation(out=n[:], in_=v[:], func=ACT.Tanh, bias=bcol[:, 2:3], scale=1.0)
             rs = work.tile([P, 512], F32, tag="rs")
-            if MULT_ON_GPSIMD:
+            if j < NU - 1:
                 nc.gpsimd.tensor_tensor(out=rs[:], in0=zc[:], in1=n[:], op=ALU.mult)
             else:
                 nc.vector.tensor_tensor(out=rs[:], in0=zc[:], in1=n[:], op=ALU.mult)
@@ -205,11 +208,15 @@ def tile_grucellmodel_pa_t_kernel(tc, input_seq, W_ih, b_ih, gh, out):
 
         def store(j):
             osb = work.tile([P, 512], F32, tag="osb")
-            nc.scalar.copy(out=osb[:], in_=pout[j][:])
+            if j < NU - 1:
+                nc.vector.tensor_copy(out=osb[:], in_=pout[j][:])
+            else:
+                nc.scalar.copy(out=osb[:], in_=pout[j][:])
             nc.sync.dma_start(out=out_view[j], in_=osb[:].rearrange("p (q f) -> p q f", q=2))
 
-        transposes(0)
-        copies(0, "vs")
+        transposes(0, psx, "xt")
+        copy_half(0, 0)
+        copy_half(0, 1)
         for g in range(3):
             nc.vector.quantize_mx(
                 out=wcodes[:, g * P : (g + 1) * P].bitcast(FP8X4),
@@ -217,38 +224,44 @@ def tile_grucellmodel_pa_t_kernel(tc, input_seq, W_ih, b_ih, gh, out):
                 in_=wgrouped[:, g * I : (g + 1) * I],
             )
         quantise(0)
-        transposes(1)
-        passes(0)
         bcol = const.tile([P, 4], F32)
-        nc.vector.tensor_copy(out=bcol[:], in_=pgh[:, 384:388])
+        nc.scalar.copy(out=bcol[:], in_=pgh[:, 384:388])
+        nbz = const.tile([P, 1], F32)
+        nc.scalar.mul(out=nbz[:], in_=pgh[:, 385:386], mul=-1.0)
         g_r = const.tile([P, P], F32)
-        nc.vector.tensor_scalar(out=g_r[:], in0=pgh[:, 0:128], scalar1=bcol[:, 0:1], scalar2=None, op0=ALU.add)
+        nc.scalar.activation(out=g_r[:], in_=pgh[:, 0:128], func=ACT.Identity, bias=bcol[:, 0:1], scale=1.0)
         g_zn = const.tile([P, P], F32)
-        nc.vector.tensor_scalar(
-            out=g_zn[:], in0=pgh[:, 128:256], scalar1=bcol[:, 1:2], scalar2=-1.0, op0=ALU.add, op1=ALU.mult
-        )
+        nc.scalar.activation(out=g_zn[:], in_=pgh[:, 128:256], func=ACT.Identity, bias=nbz[:, 0:1], scale=-1.0)
         h_n = const.tile([P, P], F32)
-        nc.vector.tensor_copy(out=h_n[:], in_=pgh[:, 256:384])
-        copies(1, "vs")
-        transposes(2)
+        nc.scalar.copy(out=h_n[:], in_=pgh[:, 256:384])
+        transposes(1, psg, "gate")
+        passes(0)
+        copy_half(1, 0)
+        copy_half(1, 1)
         quantise(1)
-        copies(2, "vs")
+        transposes(2, psx, "xt")
+        passes(1)
+        copy_half(2, 0)
+        copy_half(2, 1)
 
         for i in range(NU + 1):
-            if i + 3 < NU:
-                transposes(i + 3)
+            if i + AHEAD < NU:
+                transposes(i + AHEAD, psx, "xt")
             if i >= 1:
                 back_transposes(i - 1)
-            if i + 1 < NU:
+            if 1 <= i < NU - 1:
                 passes(i + 1)
             if i < NU:
                 reset_and_candidate(i)
-                update(i)
-            if i + 2 < NU:
-                quantise(i + 2)
-            if i + 3 < NU:
-                copies(i + 3, "vv")
+            if i + AHEAD < NU:
+                copy_half(i + AHEAD, 0)
             if i < NU:
-                candidate_and_product(i)
+                update(i)
+            if i + AHEAD - 1 < NU:
+                quantise(i + AHEAD - 1)
             if i >= 1:
                 store(i - 1)
+            if i + AHEAD < NU:
+                copy_half(i + AHEAD, 1)
+            if i < NU:
+                candidate_and_product(i)

@@ -18,6 +18,8 @@ FLOPS = 2 * T * B * I * 3 * H
 NU = 16
 CHUNKS = [2, 2, 4, 8, 8, 8, 8, 8, 8, 8]
 AHEAD = 3
+SCALAR_INPUT_COPIES = ((0, 0), (0, 1), (2, 0))
+SCALAR_RESULT_COPIES = (0, 2, 4, 6, 8, 10, 15)
 
 
 def tile_grucellmodel_pa_t_kernel(tc, input_seq, W_ih, b_ih, gh, out):
@@ -68,9 +70,6 @@ def tile_grucellmodel_pa_t_kernel(tc, input_seq, W_ih, b_ih, gh, out):
 
         ghf = const.tile([P, 512], F32)
         nc.scalar.copy(out=ghf[:], in_=ghb[:])
-        pgh = psg.tile([P, 512], F32, tag="gate")
-        for g in range(4):
-            nc.tensor.transpose(pgh[:, g * P : (g + 1) * P], ghf[:, g * P : (g + 1) * P], ident[:])
 
         ww = w_sb[:].bitcast(F32)
         pwa = psg.tile([P, 512], F32, tag="gate")
@@ -79,6 +78,9 @@ def tile_grucellmodel_pa_t_kernel(tc, input_seq, W_ih, b_ih, gh, out):
             for u in range(2):
                 dst = pwa[:, (2 * g + u) * P : (2 * g + u + 1) * P] if g < 2 else pwb[:, u * P : (u + 1) * P]
                 nc.tensor.transpose(dst, ww[:, g * 256 + u * P : g * 256 + (u + 1) * P], ident[:])
+        pgh = psg.tile([P, 512], F32, tag="gate")
+        for g in range(4):
+            nc.tensor.transpose(pgh[:, g * P : (g + 1) * P], ghf[:, g * P : (g + 1) * P], ident[:])
         wgrouped = const.tile([P, 3 * I], BF16, align_bytes=64)
         wgw = wgrouped[:].bitcast(F32)
         nc.vector.tensor_copy(
@@ -121,7 +123,7 @@ def tile_grucellmodel_pa_t_kernel(tc, input_seq, W_ih, b_ih, gh, out):
             gw = grouped[j][:].bitcast(F32)
             dst = gw[:, half * 512 : (half + 1) * 512].rearrange("p (c n u) -> p c n u", c=2, u=2)
             src = banks[j][half][:].rearrange("p (c u n) -> p c n u", c=2, u=2)
-            if half == 0 and (j == 0 or j % 2 == 1):
+            if (j, half) in SCALAR_INPUT_COPIES:
                 nc.scalar.copy(out=dst, in_=src)
             else:
                 nc.vector.tensor_copy(out=dst, in_=src)
@@ -158,7 +160,7 @@ def tile_grucellmodel_pa_t_kernel(tc, input_seq, W_ih, b_ih, gh, out):
         def reset_and_candidate(j):
             pr = gates[j][0]
             pn = gates[j][2]
-            r = work.tile([P, 512], F32, tag="r", bufs=2)
+            r = work.tile([P, 512], F32, tag="r")
             v = work.tile([P, 512], F32, tag="v")
             v5 = placed(v[:])
             for c in range(4):
@@ -189,12 +191,15 @@ def tile_grucellmodel_pa_t_kernel(tc, input_seq, W_ih, b_ih, gh, out):
                     )
             acts[j].append(zc)
 
-        def candidate_and_product(j):
-            v, zc = acts[j]
+        def candidate(j):
             n = work.tile([P, 512], F32, tag="n", bufs=2)
-            nc.scalar.activation(out=n[:], in_=v[:], func=ACT.Tanh, bias=bcol[:, 2:3], scale=1.0)
+            nc.scalar.activation(out=n[:], in_=acts[j][0][:], func=ACT.Tanh, bias=bcol[:, 2:3], scale=1.0)
+            acts[j].append(n)
+
+        def product(j):
+            v, zc, n = acts[j]
             rs = work.tile([P, 512], F32, tag="rs")
-            if j < NU - 1:
+            if j < NU - 2:
                 nc.gpsimd.tensor_tensor(out=rs[:], in0=zc[:], in1=n[:], op=ALU.mult)
             else:
                 nc.vector.tensor_tensor(out=rs[:], in0=zc[:], in1=n[:], op=ALU.mult)
@@ -208,10 +213,10 @@ def tile_grucellmodel_pa_t_kernel(tc, input_seq, W_ih, b_ih, gh, out):
 
         def store(j):
             osb = work.tile([P, 512], F32, tag="osb")
-            if j < NU - 1:
-                nc.vector.tensor_copy(out=osb[:], in_=pout[j][:])
-            else:
+            if j in SCALAR_RESULT_COPIES:
                 nc.scalar.copy(out=osb[:], in_=pout[j][:])
+            else:
+                nc.vector.tensor_copy(out=osb[:], in_=pout[j][:])
             nc.sync.dma_start(out=out_view[j], in_=osb[:].rearrange("p (q f) -> p q f", q=2))
 
         transposes(0, psx, "xt")
@@ -235,33 +240,35 @@ def tile_grucellmodel_pa_t_kernel(tc, input_seq, W_ih, b_ih, gh, out):
         h_n = const.tile([P, P], F32)
         nc.scalar.copy(out=h_n[:], in_=pgh[:, 256:384])
         transposes(1, psg, "gate")
-        passes(0)
         copy_half(1, 0)
         copy_half(1, 1)
-        quantise(1)
+        passes(0)
         transposes(2, psx, "xt")
-        passes(1)
-        copy_half(2, 0)
-        copy_half(2, 1)
 
         for i in range(NU + 1):
+            if i == 0:
+                reset_and_candidate(0)
+                quantise(1)
+                passes(1)
+                copy_half(2, 0)
+                copy_half(2, 1)
             if i + AHEAD < NU:
                 transposes(i + AHEAD, psx, "xt")
             if i >= 1:
                 back_transposes(i - 1)
             if 1 <= i < NU - 1:
                 passes(i + 1)
-            if i < NU:
+            if 1 <= i < NU:
                 reset_and_candidate(i)
-            if i + AHEAD < NU:
-                copy_half(i + AHEAD, 0)
-            if i < NU:
-                update(i)
             if i + AHEAD - 1 < NU:
                 quantise(i + AHEAD - 1)
-            if i >= 1:
-                store(i - 1)
             if i + AHEAD < NU:
+                copy_half(i + AHEAD, 0)
                 copy_half(i + AHEAD, 1)
             if i < NU:
-                candidate_and_product(i)
+                update(i)
+                candidate(i)
+            if i >= 1:
+                store(i - 1)
+            if i < NU:
+                product(i)

@@ -18,8 +18,8 @@ FLOPS = 2 * T * B * I * 3 * H
 NU = 16
 CHUNKS = [2, 2, 4, 8, 8, 8, 8, 8, 8, 8]
 AHEAD = 3
-SCALAR_INPUT_COPIES = ((0, 0), (0, 1), (2, 0))
-SCALAR_RESULT_COPIES = (0, 2, 4, 6, 8, 10, 15)
+SCALAR_INPUT_COPIES = ((0, 1), (2, 0))
+SCALAR_RESULT_COPIES = (0, 2, 4, 6, 8, 10)
 
 
 def tile_grucellmodel_pa_t_kernel(tc, input_seq, W_ih, b_ih, gh, out):
@@ -78,9 +78,6 @@ def tile_grucellmodel_pa_t_kernel(tc, input_seq, W_ih, b_ih, gh, out):
             for u in range(2):
                 dst = pwa[:, (2 * g + u) * P : (2 * g + u + 1) * P] if g < 2 else pwb[:, u * P : (u + 1) * P]
                 nc.tensor.transpose(dst, ww[:, g * 256 + u * P : g * 256 + (u + 1) * P], ident[:])
-        pgh = psg.tile([P, 512], F32, tag="gate")
-        for g in range(4):
-            nc.tensor.transpose(pgh[:, g * P : (g + 1) * P], ghf[:, g * P : (g + 1) * P], ident[:])
         wgrouped = const.tile([P, 3 * I], BF16, align_bytes=64)
         wgw = wgrouped[:].bitcast(F32)
         nc.vector.tensor_copy(
@@ -102,19 +99,20 @@ def tile_grucellmodel_pa_t_kernel(tc, input_seq, W_ih, b_ih, gh, out):
         res = {}
         pout = {}
 
+        def transposes_half(j, half, pool, tag):
+            xw, off = half_src[2 * j + half]
+            xt = pool.tile([P, 512], F32, tag=tag)
+            for c in range(2):
+                for u in range(2):
+                    w0 = off + c * 256 + u * P
+                    nc.tensor.transpose(
+                        xt[:, (2 * c + u) * P : (2 * c + u + 1) * P], xw[:, w0 : w0 + P], perm[:]
+                    )
+            banks[(j, half)] = xt
+
         def transposes(j, pool, tag):
-            pair = []
-            for half in range(2):
-                xw, off = half_src[2 * j + half]
-                xt = pool.tile([P, 512], F32, tag=tag)
-                for c in range(2):
-                    for u in range(2):
-                        w0 = off + c * 256 + u * P
-                        nc.tensor.transpose(
-                            xt[:, (2 * c + u) * P : (2 * c + u + 1) * P], xw[:, w0 : w0 + P], perm[:]
-                        )
-                pair.append(xt)
-            banks[j] = pair
+            transposes_half(j, 0, pool, tag)
+            transposes_half(j, 1, pool, tag)
 
         def copy_half(j, half):
             if half == 0:
@@ -122,7 +120,7 @@ def tile_grucellmodel_pa_t_kernel(tc, input_seq, W_ih, b_ih, gh, out):
                 grouped[j] = gr
             gw = grouped[j][:].bitcast(F32)
             dst = gw[:, half * 512 : (half + 1) * 512].rearrange("p (c n u) -> p c n u", c=2, u=2)
-            src = banks[j][half][:].rearrange("p (c u n) -> p c n u", c=2, u=2)
+            src = banks[(j, half)][:].rearrange("p (c u n) -> p c n u", c=2, u=2)
             if (j, half) in SCALAR_INPUT_COPIES:
                 nc.scalar.copy(out=dst, in_=src)
             else:
@@ -157,14 +155,14 @@ def tile_grucellmodel_pa_t_kernel(tc, input_seq, W_ih, b_ih, gh, out):
         def placed(tile_ap):
             return tile_ap.rearrange("p (q l c h) -> p q l c h", q=2, l=2, c=4)
 
-        def reset_and_candidate(j):
+        def reset_and_candidate(j, QS=(0, 1)):
             pr = gates[j][0]
             pn = gates[j][2]
             r = work.tile([P, 512], F32, tag="r")
             v = work.tile([P, 512], F32, tag="v")
             v5 = placed(v[:])
-            for c in range(4):
-                for q in range(2):
+            for q in QS:
+                for c in range(4):
                     b = q * 64 + 4 * j + c
                     c0 = c * P + q * 64
                     nc.scalar.activation(
@@ -177,33 +175,38 @@ def tile_grucellmodel_pa_t_kernel(tc, input_seq, W_ih, b_ih, gh, out):
                     )
             acts[j] = [v]
 
-        def update(j):
+        def update(j, QS=(0, 1)):
             pz = gates[j][1]
-            zc = work.tile([P, 512], F32, tag="zc")
-            z5 = placed(zc[:])
-            for c in range(4):
-                for q in range(2):
+            if QS[0] == 0:
+                zc = work.tile([P, 512], F32, tag="zc")
+                acts[j].append(zc)
+            z5 = placed(acts[j][1][:])
+            for q in QS:
+                for c in range(4):
                     b = q * 64 + 4 * j + c
                     c0 = c * P + q * 64
                     nc.scalar.activation(
                         out=z5[:, q, :, c, :], in_=split(pz[:, c0 : c0 + 64]), func=ACT.Sigmoid,
                         bias=g_zn[:, b : b + 1], scale=-1.0,
                     )
-            acts[j].append(zc)
 
-        def candidate(j):
-            n = work.tile([P, 512], F32, tag="n", bufs=2)
-            nc.scalar.activation(out=n[:], in_=acts[j][0][:], func=ACT.Tanh, bias=bcol[:, 2:3], scale=1.0)
-            acts[j].append(n)
+        def candidate(j, lo=0, hi=512):
+            if lo == 0:
+                n = work.tile([P, 512], F32, tag="n", bufs=2)
+                acts[j].append(n)
+            nc.scalar.activation(
+                out=acts[j][2][:, lo:hi], in_=acts[j][0][:, lo:hi], func=ACT.Tanh, bias=bcol[:, 2:3], scale=1.0
+            )
 
-        def product(j):
+        def product(j, lo=0, hi=512):
             v, zc, n = acts[j]
-            rs = work.tile([P, 512], F32, tag="rs")
+            if lo == 0:
+                rs = work.tile([P, 512], F32, tag="rs")
+                res[j] = rs
             if j < NU - 2:
-                nc.gpsimd.tensor_tensor(out=rs[:], in0=zc[:], in1=n[:], op=ALU.mult)
+                nc.gpsimd.tensor_tensor(out=res[j][:, lo:hi], in0=zc[:, lo:hi], in1=n[:, lo:hi], op=ALU.mult)
             else:
-                nc.vector.tensor_tensor(out=rs[:], in0=zc[:], in1=n[:], op=ALU.mult)
-            res[j] = rs
+                nc.vector.tensor_tensor(out=res[j][:, lo:hi], in0=zc[:, lo:hi], in1=n[:, lo:hi], op=ALU.mult)
 
         def back_transposes(j):
             po = pso.tile([P, 512], F32, tag="po")
@@ -219,6 +222,22 @@ def tile_grucellmodel_pa_t_kernel(tc, input_seq, W_ih, b_ih, gh, out):
                 nc.vector.tensor_copy(out=osb[:], in_=pout[j][:])
             nc.sync.dma_start(out=out_view[j], in_=osb[:].rearrange("p (q f) -> p q f", q=2))
 
+        def back_transposes_half(j, q):
+            ph = psx.tile([P, 512], F32, tag="xt")
+            for l in range(2):
+                nc.tensor.transpose(
+                    ph[:, l * P : (l + 1) * P], res[j][:, (2 * q + l) * P : (2 * q + l + 1) * P], ident[:]
+                )
+            pout[(j, q)] = ph
+
+        def store_half(j, q):
+            osh = work.tile([P, 256], F32, tag="osh", bufs=2)
+            if q == 0:
+                nc.vector.tensor_copy(out=osh[:], in_=pout[(j, q)][:, 0:256])
+            else:
+                nc.scalar.copy(out=osh[:], in_=pout[(j, q)][:, 0:256])
+            nc.sync.dma_start(out=out_view[j][:, q, :], in_=osh[:])
+
         transposes(0, psx, "xt")
         copy_half(0, 0)
         copy_half(0, 1)
@@ -229,6 +248,11 @@ def tile_grucellmodel_pa_t_kernel(tc, input_seq, W_ih, b_ih, gh, out):
                 in_=wgrouped[:, g * I : (g + 1) * I],
             )
         quantise(0)
+        transposes_half(1, 0, psg, "gate")
+        pgh = psg.tile([P, 512], F32, tag="gate")
+        for g in range(4):
+            nc.tensor.transpose(pgh[:, g * P : (g + 1) * P], ghf[:, g * P : (g + 1) * P], ident[:])
+        transposes_half(1, 1, psg, "gate")
         bcol = const.tile([P, 4], F32)
         nc.scalar.copy(out=bcol[:], in_=pgh[:, 384:388])
         nbz = const.tile([P, 1], F32)
@@ -239,36 +263,47 @@ def tile_grucellmodel_pa_t_kernel(tc, input_seq, W_ih, b_ih, gh, out):
         nc.scalar.activation(out=g_zn[:], in_=pgh[:, 128:256], func=ACT.Identity, bias=nbz[:, 0:1], scale=-1.0)
         h_n = const.tile([P, P], F32)
         nc.scalar.copy(out=h_n[:], in_=pgh[:, 256:384])
-        transposes(1, psg, "gate")
         copy_half(1, 0)
         copy_half(1, 1)
+        quantise(1)
         passes(0)
         transposes(2, psx, "xt")
+        passes(1)
 
-        for i in range(NU + 1):
+        LAST = NU - 1
+        for i in range(NU):
             if i == 0:
                 reset_and_candidate(0)
-                quantise(1)
-                passes(1)
                 copy_half(2, 0)
                 copy_half(2, 1)
             if i + AHEAD < NU:
                 transposes(i + AHEAD, psx, "xt")
             if i >= 1:
                 back_transposes(i - 1)
-            if 1 <= i < NU - 1:
+            if 1 <= i < LAST:
                 passes(i + 1)
-            if 1 <= i < NU:
+            if i >= 1:
                 reset_and_candidate(i)
             if i + AHEAD - 1 < NU:
                 quantise(i + AHEAD - 1)
             if i + AHEAD < NU:
                 copy_half(i + AHEAD, 0)
                 copy_half(i + AHEAD, 1)
-            if i < NU:
+            if i < LAST:
                 update(i)
                 candidate(i)
+            else:
+                update(i, (0,))
+                candidate(i, 0, 256)
             if i >= 1:
                 store(i - 1)
-            if i < NU:
+            if i < LAST:
                 product(i)
+        product(LAST, 0, 256)
+        update(LAST, (1,))
+        candidate(LAST, 256, 512)
+        product(LAST, 256, 512)
+        back_transposes_half(LAST, 0)
+        back_transposes_half(LAST, 1)
+        store_half(LAST, 0)
+        store_half(LAST, 1)

@@ -34,6 +34,16 @@ def tile_grucellmodel_pa_t_kernel(tc, input_seq, W_ih, b_ih, gh, out):
         pso = ctx.enter_context(tc.psum_pool(name="pso", bufs=1))
         ctx.enter_context(tc.manual_schedule())
 
+        zeros = const.tile([P, 512], BF16)
+        nc.vector.memset(zeros[:], 0.0)
+        pwarm = pso.tile([P, 512], F32, tag="po")
+
+        def idle_matmuls(count):
+            for k in range(count):
+                nc.tensor.matmul(out=pwarm[:], lhsT=zeros[:, 0:P], rhs=zeros[:], start=True, stop=True)
+
+        idle_matmuls(8)
+
         ghb = const.tile([P, 512], BF16)
         nc.vector.memset(ghb[:, 384:512], 0.0)
         nc.scalar.dma_start(out=ghb[:, 0:384], in_=gh)
@@ -239,6 +249,7 @@ def tile_grucellmodel_pa_t_kernel(tc, input_seq, W_ih, b_ih, gh, out):
             nc.sync.dma_start(out=out_view[j][:, q, :], in_=osh[:])
 
         transposes(0, psx, "xt")
+        idle_matmuls(2)
         copy_half(0, 0)
         copy_half(0, 1)
         for g in range(3):
@@ -253,6 +264,7 @@ def tile_grucellmodel_pa_t_kernel(tc, input_seq, W_ih, b_ih, gh, out):
         for g in range(4):
             nc.tensor.transpose(pgh[:, g * P : (g + 1) * P], ghf[:, g * P : (g + 1) * P], ident[:])
         transposes_half(1, 1, psg, "gate")
+        idle_matmuls(2)
         bcol = const.tile([P, 4], F32)
         nc.scalar.copy(out=bcol[:], in_=pgh[:, 384:388])
         nbz = const.tile([P, 1], F32)

from contextlib import ExitStack

import concourse.mybir as mybir
from concourse.masks import make_identity

F32 = mybir.dt.float32
BF16 = mybir.dt.bfloat16
U32 = mybir.dt.uint32
U8 = mybir.dt.uint8
FP8X4 = mybir.dt.float8_e4m3fn_x4
ACT = mybir.ActivationFunctionType
ALU = mybir.AluOpType

T, B, I, H = 64, 128, 512, 128
P = 128
FLOPS = 2 * T * B * I * 3 * H

NU = 16
CHUNKS = [2, 2, 4, 8, 8, 8, 8, 8, 8, 8]
AHEAD = 3
SCALAR_INPUT_COPIES = ((0, 1), (2, 0))
SCALAR_RESULT_COPIES = (0, 2, 4, 6, 8, 10)


def tile_grucellmodel_pa_t_kernel(tc, input_seq, W_ih, b_ih, gh, out):
    nc = tc.nc
    with ExitStack() as ctx:
        const = ctx.enter_context(tc.tile_pool(name="const", bufs=1))
        xpool = ctx.enter_context(tc.tile_pool(name="xpool", bufs=1))
        gpool = ctx.enter_context(tc.tile_pool(name="gpool", bufs=4))
        work = ctx.enter_context(tc.tile_pool(name="work", bufs=3))
        psx = ctx.enter_context(tc.psum_pool(name="psx", bufs=2))
        psg = ctx.enter_context(tc.psum_pool(name="psg", bufs=5))
        pso = ctx.enter_context(tc.psum_pool(name="pso", bufs=1))
        ctx.enter_context(tc.manual_schedule())

        zeros = const.tile([P, 512], BF16)
        nc.vector.memset(zeros[:], 0.0)
        pwarm = pso.tile([P, 512], F32, tag="po")

        def idle_matmuls(count):
            for k in range(count):
                nc.tensor.matmul(out=pwarm[:], lhsT=zeros[:, 0:P], rhs=zeros[:], start=True, stop=True)

        idle_matmuls(8)

        ghb = const.tile([P, 512], BF16)
        nc.vector.memset(ghb[:, 384:512], 0.0)
        nc.scalar.dma_start(out=ghb[:, 0:384], in_=gh)
        nc.scalar.dma_start(out=ghb[0:3, 384:512], in_=b_ih.rearrange("(g h) -> g h", g=3))
        warm = const.tile([P, 1], F32)
        nc.vector.memset(warm[:], 0.0)
        warm2 = const.tile([P, 1], F32)
        nc.scalar.activation(out=warm2[:], in_=warm[:], func=ACT.Sigmoid)
        w_sb = const.tile([P, 3 * I], BF16)
        nc.sync.dma_start(
            out=w_sb[:].rearrange("p (g k) -> p g k", g=3),
            in_=W_ih.rearrange("(g p) k -> p g k", g=3),
        )
        xflat = input_seq.rearrange("t b k -> (t b k)").rearrange("(p f) -> p f", p=P)
        half_src = []
        bb0 = 0
        for c, nbb in enumerate(CHUNKS):
            xc = xpool.tile([P, nbb * I], BF16, name="x%d" % c)
            nc.sync.dma_start(out=xc[:], in_=xflat[:, bb0 * I : (bb0 + nbb) * I])
            for s in range(nbb // 2):
                half_src.append((xc[:].bitcast(F32), s * 2 * 256))
            bb0 += nbb
        out_view = out.rearrange("b t h -> (b t h)").rearrange(
            "(q j i f) -> j i q f", q=2, j=NU, i=P
        )

        ident = const.tile([P, P], F32)
        make_identity(nc, ident[:])
        perm = const.tile([P, P], F32)
        nc.vector.tensor_copy(
            out=perm[:].rearrange("p (q l h) -> p q l h", q=2, l=2),
            in_=ident[:].rearrange("p (h l q) -> p q l h", q=2, l=2),
        )

        ghf = const.tile([P, 512], F32)
        nc.scalar.copy(out=ghf[:], in_=ghb[:])

        ww = w_sb[:].bitcast(F32)
        pwa = psg.tile([P, 512], F32, tag="gate")
        pwb = psg.tile([P, 512], F32, tag="gate")
        for g in range(3):
            for u in range(2):
                dst = pwa[:, (2 * g + u) * P : (2 * g + u + 1) * P] if g < 2 else pwb[:, u * P : (u + 1) * P]
                nc.tensor.transpose(dst, ww[:, g * 256 + u * P : g * 256 + (u + 1) * P], ident[:])
        wgrouped = const.tile([P, 3 * I], BF16, align_bytes=64)
        wgw = wgrouped[:].bitcast(F32)
        nc.vector.tensor_copy(
            out=wgw[:, 0:512].rearrange("p (c n u) -> p c n u", c=2, u=2),
            in_=pwa[:].rearrange("p (c u n) -> p c n u", c=2, u=2),
        )
        nc.scalar.copy(
            out=wgw[:, 512:768].rearrange("p (n u) -> p n u", u=2),
            in_=pwb[:, 0:256].rearrange("p (u n) -> p n u", u=2),
        )
        wcodes = const.tile([P, 3 * P], U32, align_bytes=64)
        wscales = const.tile([P, 3 * P], U8, align_bytes=64)

        banks = {}
        grouped = {}
        codes = {}
        gates = {}
        acts = {}
        res = {}
        pout = {}

        def transposes_half(j, half, pool, tag):
            xw, off = half_src[2 * j + half]
            xt = pool.tile([P, 512], F32, tag=tag)
            for c in range(2):
                for u in range(2):
                    w0 = off + c * 256 + u * P
                    nc.tensor.transpose(
                        xt[:, (2 * c + u) * P : (2 * c + u + 1) * P], xw[:, w0 : w0 + P], perm[:]
                    )
            banks[(j, half)] = xt

        def transposes(j, pool, tag):
            transposes_half(j, 0, pool, tag)
            transposes_half(j, 1, pool, tag)

        def copy_half(j, half):
            if half == 0:
                gr = gpool.tile([P, 2048], BF16, tag="grouped", align_bytes=64, bufs=3)
                grouped[j] = gr
            gw = grouped[j][:].bitcast(F32)
            dst = gw[:, half * 512 : (half + 1) * 512].rearrange("p (c n u) -> p c n u", c=2, u=2)
            src = banks[(j, half)][:].rearrange("p (c u n) -> p c n u", c=2, u=2)
            if (j, half) in SCALAR_INPUT_COPIES:
                nc.scalar.copy(out=dst, in_=src)
            else:
                nc.vector.tensor_copy(out=dst, in_=src)

        def quantise(j):
            cd = gpool.tile([P, 512], U32, tag="codes", align_bytes=64)
            sc = gpool.tile([P, 512], U8, tag="scales", align_bytes=64)
            nc.vector.quantize_mx(out=cd[:].bitcast(FP8X4), scales=sc[:], in_=grouped[j][:])
            codes[j] = (cd, sc)

        def passes(j):
            cd, sc = codes[j]
            trio = {}
            for g in (0, 2, 1):
                pg = psg.tile([P, 512], F32, tag="gate")
                nc.tensor.matmul_mx(
                    out=pg[:],
                    lhsT=wcodes[:, g * P : (g + 1) * P].bitcast(FP8X4),
                    lhsT_scale=wscales[:, g * P : (g + 1) * P],
                    rhs=cd[:].bitcast(FP8X4),
                    rhs_scale=sc[:],
                    start=True,
                    stop=True,
                )
                trio[g] = pg
            gates[j] = trio

        def split(ap):
            return ap.rearrange("p (l h) -> p l h", l=2)

        def placed(tile_ap):
            return tile_ap.rearrange("p (q l c h) -> p q l c h", q=2, l=2, c=4)

        def reset_and_candidate(j, QS=(0, 1)):
            pr = gates[j][0]
            pn = gates[j][2]
            r = work.tile([P, 512], F32, tag="r")
            v = work.tile([P, 512], F32, tag="v")
            v5 = placed(v[:])
            for q in QS:
                for c in range(4):
                    b = q * 64 + 4 * j + c
                    c0 = c * P + q * 64
                    nc.scalar.activation(
                        out=r[:, c0 : c0 + 64], in_=pr[:, c0 : c0 + 64], func=ACT.Sigmoid,
                        bias=g_r[:, b : b + 1], scale=1.0,
                    )
                    nc.vector.scalar_tensor_tensor(
                        out=v5[:, q, :, c, :], in0=split(r[:, c0 : c0 + 64]), scalar=h_n[:, b : b + 1],
                        in1=split(pn[:, c0 : c0 + 64]), op0=ALU.mult, op1=ALU.add,
                    )
            acts[j] = [v]

        def update(j, QS=(0, 1)):
            pz = gates[j][1]
            if QS[0] == 0:
                zc = work.tile([P, 512], F32, tag="zc")
                acts[j].append(zc)
            z5 = placed(acts[j][1][:])
            for q in QS:
                for c in range(4):
                    b = q * 64 + 4 * j + c
                    c0 = c * P + q * 64
                    nc.scalar.activation(
                        out=z5[:, q, :, c, :], in_=split(pz[:, c0 : c0 + 64]), func=ACT.Sigmoid,
                        bias=g_zn[:, b : b + 1], scale=-1.0,
                    )

        def candidate(j, lo=0, hi=512):
            if lo == 0:
                n = work.tile([P, 512], F32, tag="n", bufs=2)
                acts[j].append(n)
            nc.scalar.activation(
                out=acts[j][2][:, lo:hi], in_=acts[j][0][:, lo:hi], func=ACT.Tanh, bias=bcol[:, 2:3], scale=1.0
            )

        def product(j, lo=0, hi=512):
            v, zc, n = acts[j]
            if lo == 0:
                rs = work.tile([P, 512], F32, tag="rs")
                res[j] = rs
            if j < NU - 2:
                nc.gpsimd.tensor_tensor(out=res[j][:, lo:hi], in0=zc[:, lo:hi], in1=n[:, lo:hi], op=ALU.mult)
            else:
                nc.vector.tensor_tensor(out=res[j][:, lo:hi], in0=zc[:, lo:hi], in1=n[:, lo:hi], op=ALU.mult)

        def back_transposes(j):
            po = pso.tile([P, 512], F32, tag="po")
            for q in range(4):
                nc.tensor.transpose(po[:, q * P : (q + 1) * P], res[j][:, q * P : (q + 1) * P], ident[:])
            pout[j] = po

        def store(j):
            osb = work.tile([P, 512], F32, tag="osb")
            if j in SCALAR_RESULT_COPIES:
                nc.scalar.copy(out=osb[:], in_=pout[j][:])
            else:
                nc.vector.tensor_copy(out=osb[:], in_=pout[j][:])
            nc.sync.dma_start(out=out_view[j], in_=osb[:].rearrange("p (q f) -> p q f", q=2))

        def back_transposes_half(j, q):
            ph = psx.tile([P, 512], F32, tag="xt")
            for l in range(2):
                nc.tensor.transpose(
                    ph[:, l * P : (l + 1) * P], res[j][:, (2 * q + l) * P : (2 * q + l + 1) * P], ident[:]
                )
            pout[(j, q)] = ph

        def store_half(j, q):
            osh = work.tile([P, 256], F32, tag="osh", bufs=2)
            if q == 0:
                nc.vector.tensor_copy(out=osh[:], in_=pout[(j, q)][:, 0:256])
            else:
                nc.scalar.copy(out=osh[:], in_=pout[(j, q)][:, 0:256])
            nc.sync.dma_start(out=out_view[j][:, q, :], in_=osh[:])

        transposes(0, psx, "xt")
        idle_matmuls(2)
        copy_half(0, 0)
        copy_half(0, 1)
        for g in range(3):
            nc.vector.quantize_mx(
                out=wcodes[:, g * P : (g + 1) * P].bitcast(FP8X4),
                scales=wscales[:, g * P : (g + 1) * P],
                in_=wgrouped[:, g * I : (g + 1) * I],
            )
        quantise(0)
        transposes_half(1, 0, psg, "gate")
        pgh = psg.tile([P, 512], F32, tag="gate")
        for g in range(4):
            nc.tensor.transpose(pgh[:, g * P : (g + 1) * P], ghf[:, g * P : (g + 1) * P], ident[:])
        transposes_half(1, 1, psg, "gate")
        idle_matmuls(2)
        bcol = const.tile([P, 4], F32)
        nc.scalar.copy(out=bcol[:], in_=pgh[:, 384:388])
        nbz = const.tile([P, 1], F32)
        nc.scalar.mul(out=nbz[:], in_=pgh[:, 385:386], mul=-1.0)
        g_r = const.tile([P, P], F32)
        nc.scalar.activation(out=g_r[:], in_=pgh[:, 0:128], func=ACT.Identity, bias=bcol[:, 0:1], scale=1.0)
        g_zn = const.tile([P, P], F32)
        nc.scalar.activation(out=g_zn[:], in_=pgh[:, 128:256], func=ACT.Identity, bias=nbz[:, 0:1], scale=-1.0)
        h_n = const.tile([P, P], F32)
        nc.scalar.copy(out=h_n[:], in_=pgh[:, 256:384])
        copy_half(1, 0)
        copy_half(1, 1)
        quantise(1)
        passes(0)
        transposes(2, psx, "xt")
        passes(1)

        LAST = NU - 1
        for i in range(NU):
            if i == 0:
                reset_and_candidate(0)
                copy_half(2, 0)
                copy_half(2, 1)
            if i + AHEAD < NU:
                transposes(i + AHEAD, psx, "xt")
            if i >= 1:
                back_transposes(i - 1)
            if 1 <= i < LAST:
                passes(i + 1)
            if i >= 1:
                reset_and_candidate(i)
            if i + AHEAD - 1 < NU:
                quantise(i + AHEAD - 1)
            if i + AHEAD < NU:
                copy_half(i + AHEAD, 0)
                copy_half(i + AHEAD, 1)
            if i < LAST:
                update(i)
                candidate(i)
            else:
                update(i, (0,))
                candidate(i, 0, 256)
            if i >= 1:
                store(i - 1)
            if i < LAST:
                product(i)
        product(LAST, 0, 256)
        update(LAST, (1,))
        candidate(LAST, 256, 512)
        product(LAST, 256, 512)
        back_transposes_half(LAST, 0)
        back_transposes_half(LAST, 1)
        store_half(LAST, 0)
        store_half(LAST, 1)
